import numpy as np
import ml_dtypes


def mxq(x, axis, fmt="e4m3"):
    dtype, down = {"e4m3": (ml_dtypes.float8_e4m3fn, 7), "e5m2": (ml_dtypes.float8_e5m2, 14)}[fmt]
    v = np.moveaxis(np.asarray(x, np.float32).astype(ml_dtypes.bfloat16).astype(np.float64), axis, -1)
    blocks = v.reshape(v.shape[:-1] + (-1, 32))
    amax = np.abs(blocks).max(-1, keepdims=True)
    byte = np.maximum(np.where(amax > 0, np.frexp(amax)[1] - 1 + 127, 0) - down, 1)
    scale = np.exp2(byte - 127.0)
    codes = (blocks / scale).astype(np.float32).astype(dtype).astype(np.float64)
    return np.moveaxis((codes * scale).reshape(v.shape), -1, axis)


WIDE = False


def mx_kscale(k):
    if not WIDE:
        return np.ones(k)
    levels = np.array([10, -10, 5, -5, 0])
    a = np.random.permutation(np.resize(levels, k // 512 * 4)).reshape(k // 512, 4)
    idx = np.arange(k)
    return np.exp2(a[idx // 512, idx % 128 // 32])


BF16 = ml_dtypes.bfloat16


def bf(x):
    return np.asarray(x, np.float32).astype(BF16)


def f64(x):
    return np.asarray(x).astype(np.float64)


B, SIDE, HE, Z, HD, XO = 128, 32, 512, 8192, 1024, 1024


def setup_inputs():
    n = np.random.standard_normal
    s, t = mx_kscale(HE), mx_kscale(Z)
    return {"h": bf(np.tanh(n((B, HE))) * s),
            "W_mu_e": bf(n((Z, HE)) * 1.5 / np.sqrt(HE) / s[None, :] * t[:, None]),
            "b_mu_e": bf(n(Z) * 0.3 * t),
            "W_ls_e": bf(n((Z, HE)) * 1.5 / np.sqrt(HE) / s[None, :]),
            "b_ls_e": bf(n(Z) * 0.3),
            "eps_z": bf(n((B, Z)) * t),
            "W_in_d": bf(n((HD, Z)) * 0.6 / np.sqrt(Z) / t[None, :]),
            "b_in_d": bf(n(HD) * 0.3)}


def reference(h, W_mu_e, b_mu_e, W_ls_e, b_ls_e, eps_z, W_in_d, b_in_d):
    hq = mxq(f64(h), 1, "e4m3")
    mu_e = (hq @ mxq(f64(W_mu_e), 1, "e4m3").T) + f64(b_mu_e)
    ls_e = (hq @ mxq(f64(W_ls_e), 1, "e4m3").T) + f64(b_ls_e)
    z = mu_e + np.exp(0.5 * ls_e) * f64(eps_z)
    return np.tanh((mxq(z, 1, "e4m3") @ mxq(f64(W_in_d), 1, "e4m3").T) + f64(b_in_d))

@@ -1,0 +1,280 @@
+from contextlib import ExitStack
+
+import concourse.mybir as mybir
+from concourse.masks import make_identity
+
+F32 = mybir.dt.float32
+BF16 = mybir.dt.bfloat16
+U32 = mybir.dt.uint32
+U8 = mybir.dt.uint8
+FP8X4 = mybir.dt.float8_e4m3fn_x4
+ACT = mybir.ActivationFunctionType
+ALU = mybir.AluOpType
+
+P = 128
+PACK = 4
+K_PASS = P * PACK
+HIDDEN = 512
+LATENT = 8192
+OUT = 1024
+Z_PASSES = LATENT // K_PASS
+N_BLOCKS = OUT // P
+UNIT_WORDS = 8 * P
+STEPS = Z_PASSES + 2 * N_BLOCKS
+W_BUFS = 6
+D_BUFS = 5
+
+FLOPS = 2 * P * (2 * HIDDEN * LATENT + LATENT * OUT)
+
+
+def tile_vae_pa_k_kernel(tc, h, W_mu_e, b_mu_e, W_ls_e, b_ls_e, eps_z, W_in_d, b_in_d, out):
+    nc = tc.nc
+    with ExitStack() as ctx:
+        ctx.enter_context(tc.manual_schedule())
+        keep = ctx.enter_context(tc.tile_pool(name="keep", bufs=1))
+        w_pool = ctx.enter_context(tc.tile_pool(name="w_pool", bufs=W_BUFS))
+        d_pool = ctx.enter_context(tc.tile_pool(name="d_pool", bufs=D_BUFS))
+        grouped_pool = ctx.enter_context(tc.tile_pool(name="grouped_pool", bufs=4))
+        packed_pool = ctx.enter_context(tc.tile_pool(name="packed_pool", bufs=4))
+        sample_pool = ctx.enter_context(tc.tile_pool(name="sample_pool", bufs=2))
+        xt_pool = ctx.enter_context(tc.psum_pool(name="xt_pool", bufs=4))
+        acc_pool = ctx.enter_context(tc.psum_pool(name="acc_pool", bufs=2))
+        ls_pool = ctx.enter_context(tc.psum_pool(name="ls_pool", bufs=1))
+        eps_pool = ctx.enter_context(tc.psum_pool(name="eps_pool", bufs=1))
+
+        ident = keep.tile([P, P], F32)
+        make_identity(nc, ident[:])
+        ones = keep.tile([P, P], BF16)
+        nc.vector.memset(ones[:], 1.0)
+        bias_rows = keep.tile([P, 2 * P], BF16)
+        nc.vector.memset(bias_rows[:], 0.0)
+        b_in_row = keep.tile([P, OUT], BF16)
+        nc.vector.memset(b_in_row[:], 0.0)
+
+        h_raw = keep.tile([P, HIDDEN], BF16)
+        nc.sync.dma_start(out=h_raw[:], in_=h[:, :])
+        eps_raw = keep.tile([P, LATENT], BF16)
+        mu_rows = W_mu_e.rearrange("(c p e) k -> p c (e k)", p=P, e=2)
+        ls_rows = W_ls_e.rearrange("(c p e) k -> p c (e k)", p=P, e=2)
+        w_raw = {}
+        for g in range(Z_PASSES):
+            w_raw[g] = w_pool.tile([P, 2, 2, 2 * HIDDEN], BF16, name="w_raw")
+            nc.sync.dma_start(out=w_raw[g][:, 0, :, :], in_=mu_rows[:, 2 * g : 2 * g + 2, :])
+            nc.sync.dma_start(out=w_raw[g][:, 1, :, :], in_=ls_rows[:, 2 * g : 2 * g + 2, :])
+            if g == 0:
+                nc.sync.dma_start(out=bias_rows[0:32, :], in_=b_mu_e.rearrange("(c x) -> c x", x=2 * P))
+                nc.sync.dma_start(out=bias_rows[32:64, :], in_=b_ls_e.rearrange("(c x) -> c x", x=2 * P))
+                nc.sync.dma_start(out=b_in_row[0:1, :], in_=b_in_d.rearrange("(o n) -> o n", o=1))
+            if g % 4 == 0:
+                quarter = slice(g * K_PASS, (g + 4) * K_PASS)
+                nc.sync.dma_start(out=eps_raw[:, quarter], in_=eps_z[:, quarter])
+        d_raw = {}
+        for nb in range(N_BLOCKS):
+            d_raw[nb] = d_pool.tile([P, LATENT], BF16, name="d_raw")
+            for half in range(2):
+                cols = slice(half * LATENT // 2, (half + 1) * LATENT // 2)
+                nc.sync.dma_start(out=d_raw[nb][:, cols], in_=W_in_d[nb * P : (nb + 1) * P, cols])
+
+        def transpose_unit(words, last_copy_on_vector):
+            grouped = grouped_pool.tile([P, PACK * K_PASS], BF16, align_bytes=64)
+            grouped_words = grouped[:].bitcast(F32).rearrange("q (j c half) -> q j c half", j=4, half=2)
+            for bank in range(2):
+                xt = xt_pool.tile([P, 2, 2, P], F32)
+                for j in range(2):
+                    for half in range(2):
+                        first = ((2 * bank + j) * 2 + half) * P
+                        nc.tensor.transpose(xt[:, j, half, :], words[:, first : first + P], ident[:])
+                copy_out = nc.vector.tensor_copy if (last_copy_on_vector and bank == 1) else nc.scalar.copy
+                copy_out(
+                    out=grouped_words[:, 2 * bank : 2 * bank + 2, :, :],
+                    in_=xt[:].rearrange("q j half c -> q j c half"),
+                )
+            return grouped
+
+        def quantise_unit(grouped):
+            codes = packed_pool.tile([P, K_PASS], U32, align_bytes=64)
+            scales = packed_pool.tile([P, K_PASS], U8, align_bytes=64)
+            nc.vector.quantize_mx(out=codes[:].bitcast(FP8X4), scales=scales[:], in_=grouped[:])
+            return codes, scales
+
+        def step_units(step):
+            if step < Z_PASSES:
+                return [w_raw[step][:, w, :, :].rearrange("p c x -> p (c x)").bitcast(F32) for w in range(2)]
+            nb, half = divmod(step - Z_PASSES, 2)
+            d_words = d_raw[nb][:].bitcast(F32)
+            return [d_words[:, (2 * half + r) * UNIT_WORDS : (2 * half + r + 1) * UNIT_WORDS] for r in range(2)]
+
+        grouped_of = {}
+        packed_of = {}
+
+        def transposes(step):
+            units = step_units(step)
+            grouped_of[step] = [
+                transpose_unit(units[0], False),
+                transpose_unit(units[1], step >= Z_PASSES),
+            ]
+
+        h_words = h_raw[:].bitcast(F32)
+        h_xt = xt_pool.tile([P, 2, 2, P], F32, tag="xt")
+        for half in range(2):
+            nc.tensor.transpose(h_xt[:, 0, half, :], h_words[:, half * P : (half + 1) * P], ident[:])
+        h_grouped = keep.tile([P, K_PASS], BF16, align_bytes=64)
+        nc.vector.tensor_copy(
+            out=h_grouped[:].bitcast(F32).rearrange("q (c half) -> q c half", half=2),
+            in_=h_xt[:, 0, :, :].rearrange("q half c -> q c half"),
+        )
+        transposes(0)
+        h_codes = keep.tile([P, P], U32, align_bytes=64)
+        h_scales = keep.tile([P, P], U8, align_bytes=64)
+        nc.vector.quantize_mx(out=h_codes[:].bitcast(FP8X4), scales=h_scales[:], in_=h_grouped[:])
+
+        bias_xt = xt_pool.tile([P, 2, 2, P], F32, tag="xt")
+        nc.tensor.transpose(bias_xt[:, 0, 0, :], bias_rows[:].bitcast(F32), ident[:])
+        bias_pairs = bias_xt[:, 0, 0, :].bitcast(BF16)
+        b_mu_cols = keep.tile([P, PACK * Z_PASSES], F32)
+        nc.vector.tensor_copy(out=b_mu_cols[:], in_=bias_pairs[:, 0 : PACK * Z_PASSES])
+        half_b_ls_cols = keep.tile([P, PACK * Z_PASSES], F32)
+        nc.vector.tensor_scalar_mul(
+            out=half_b_ls_cols[:], in0=bias_pairs[:, PACK * Z_PASSES : 2 * PACK * Z_PASSES], scalar1=0.5
+        )
+
+        b_in_all = keep.tile([P, OUT], F32)
+        for half in range(2):
+            cols = slice(half * K_PASS, (half + 1) * K_PASS)
+            b_in_ps = xt_pool.tile([P, 2, 2, P], F32, tag="xt")
+            b_in_flat = b_in_ps[:].rearrange("q j half c -> q (j half c)")
+            nc.tensor.matmul(out=b_in_flat, lhsT=ones[:], rhs=b_in_row[:, cols], start=True, stop=True)
+            nc.vector.tensor_copy(out=b_in_all[:, cols], in_=b_in_flat)
+
+        packed_of[0] = [quantise_unit(grouped_of[0][0]), quantise_unit(grouped_of[0][1])]
+
+        eps_words = eps_raw[:].bitcast(F32)
+        z_codes = keep.tile([P, Z_PASSES, P], U32, align_bytes=64)
+        z_scales = keep.tile([P, Z_PASSES, P], U8, align_bytes=64)
+        pre_tanh = keep.tile([P, OUT], F32)
+        result = keep.tile([P, OUT], F32)
+        mu_of = {}
+        ls_of = {}
+        eps_of = {}
+        std_of = {}
+        noise_of = {}
+        planes_of = {}
+        z_grouped_of = {}
+        out_ps = {}
+
+        def encode(g):
+            eps_of[g] = eps_pool.tile([P, 2, P], F32, name="eps_ps")
+            for half in range(2):
+                first = (2 * g + half) * P
+                nc.tensor.transpose(eps_of[g][:, half, :], eps_words[:, first : first + P], ident[:])
+            mu_of[g] = acc_pool.tile([P, PACK, P], F32, name="mu_ps", tag="acc")
+            ls_of[g] = ls_pool.tile([P, PACK, P], F32, name="ls_ps")
+            for (codes, scales), ps in zip(packed_of[g], (mu_of[g], ls_of[g])):
+                for t in range(PACK):
+                    cols = slice(t * P, (t + 1) * P)
+                    nc.tensor.matmul_mx(
+                        out=ps[:, t, :],
+                        lhsT=codes[:, cols].bitcast(FP8X4),
+                        lhsT_scale=scales[:, cols],
+                        rhs=h_codes[:].bitcast(FP8X4),
+                        rhs_scale=h_scales[:],
+                        start=True,
+                        stop=True,
+                    )
+
+        def std_dev(g):
+            std_of[g] = sample_pool.tile([P, PACK, P], F32, name="std")
+            for t in range(PACK):
+                nc.scalar.activation(
+                    out=std_of[g][:, t, :],
+                    in_=ls_of[g][:, t, :],
+                    func=ACT.Exp,
+                    bias=half_b_ls_cols[:, PACK * g + t : PACK * g + t + 1],
+                    scale=0.5,
+                )
+
+        def scale_noise(g):
+            noise_of[g] = sample_pool.tile([P, PACK, P], F32, name="noise")
+            nc.vector.tensor_tensor(
+                out=noise_of[g][:].rearrange("p (half e) b -> p half e b", e=2),
+                in0=std_of[g][:].rearrange("p (half e) b -> p half e b", e=2),
+                in1=eps_of[g][:].bitcast(BF16).rearrange("p half (b e) -> p half e b", e=2),
+                op=ALU.mult,
+            )
+
+        def add_mean(g):
+            planes_of[g] = sample_pool.tile([P, PACK, P], BF16, name="z_planes")
+            for t in range(PACK):
+                nc.vector.scalar_tensor_tensor(
+                    out=planes_of[g][:, t, :],
+                    in0=mu_of[g][:, t, :],
+                    scalar=b_mu_cols[:, PACK * g + t : PACK * g + t + 1],
+                    in1=noise_of[g][:, t, :],
+                    op0=ALU.add,
+                    op1=ALU.add,
+                )
+
+        def regroup_z(g):
+            z_grouped_of[g] = sample_pool.tile([P, P, PACK], BF16, name="z_grouped", align_bytes=64)
+            nc.vector.tensor_copy(out=z_grouped_of[g][:], in_=planes_of[g][:].rearrange("p t b -> p b t"))
+
+        def quantise_z(g):
+            nc.vector.quantize_mx(
+                out=z_codes[:, g, :].bitcast(FP8X4),
+                scales=z_scales[:, g, :],
+                in_=z_grouped_of[g][:].rearrange("p b t -> p (b t)"),
+            )
+
+        def decode(nb, half):
+            if nb not in out_ps:
+                if nb < 2:
+                    out_ps[nb] = acc_pool.tile([P, N_BLOCKS // 2, P], F32, name="out_ps", tag="acc")
+                else:
+                    out_ps[nb] = out_ps[nb - 2]
+            for r in range(2):
+                codes, scales = packed_of[Z_PASSES + 2 * nb + half][r]
+                for j in range(PACK):
+                    g = (2 * half + r) * PACK + j
+                    cols = slice(j * P, (j + 1) * P)
+                    nc.tensor.matmul_mx(
+                        out=out_ps[nb][:, nb // 2, :],
+                        lhsT=z_codes[:, g, :].bitcast(FP8X4),
+                        lhsT_scale=z_scales[:, g, :],
+                        rhs=codes[:, cols].bitcast(FP8X4),
+                        rhs_scale=scales[:, cols],
+                        start=(g == 0),
+                        stop=(g == Z_PASSES - 1),
+                    )
+
+        def finish(nb):
+            cols = slice(nb * P, (nb + 1) * P)
+            nc.vector.tensor_tensor(
+                out=pre_tanh[:, cols], in0=out_ps[nb][:, nb // 2, :], in1=b_in_all[:, cols], op=ALU.add
+            )
+            nc.scalar.activation(out=result[:, cols], in_=pre_tanh[:, cols], func=ACT.Tanh)
+            nc.sync.dma_start(out=out[:, cols], in_=result[:, cols])
+
+        for i in range(STEPS):
+            sampling = 1 <= i <= Z_PASSES
+            if i + 1 < STEPS:
+                transposes(i + 1)
+            if sampling:
+                scale_noise(i - 1)
+            if 2 <= i <= Z_PASSES + 1:
+                quantise_z(i - 2)
+            if i < Z_PASSES:
+                encode(i)
+            else:
+                decode((i - Z_PASSES) // 2, (i - Z_PASSES) % 2)
+            if sampling:
+                add_mean(i - 1)
+            if i + 1 < STEPS:
+                first_unit = quantise_unit(grouped_of[i + 1][0])
+            if sampling:
+                regroup_z(i - 1)
+            if i + 1 < STEPS:
+                packed_of[i + 1] = [first_unit, quantise_unit(grouped_of[i + 1][1])]
+            if i < Z_PASSES:
+                std_dev(i)
+            elif (i - Z_PASSES) % 2 == 1:
+                finish((i - Z_PASSES) // 2)

@@ -18,11 +18,13 @@ HIDDEN = 512
 LATENT = 8192
 OUT = 1024
 Z_PASSES = LATENT // K_PASS
-N_BLOCKS = OUT // P
-UNIT_WORDS = 8 * P
-STEPS = Z_PASSES + 2 * N_BLOCKS
+N_TILE = 512
+N_HALVES = OUT // N_TILE
+CHUNK_PASSES = 4
+LEAD = 3
+ROUNDS = Z_PASSES + LEAD + 1
 W_BUFS = 6
-D_BUFS = 5
+D_BUFS = 4
 
 FLOPS = 2 * P * (2 * HIDDEN * LATENT + LATENT * OUT)
 
@@ -34,11 +36,12 @@ def tile_vae_pa_k_kernel(tc, h, W_mu_e, b_mu_e, W_ls_e, b_ls_e, eps_z, W_in_d, b
         keep = ctx.enter_context(tc.tile_pool(name="keep", bufs=1))
         w_pool = ctx.enter_context(tc.tile_pool(name="w_pool", bufs=W_BUFS))
         d_pool = ctx.enter_context(tc.tile_pool(name="d_pool", bufs=D_BUFS))
-        grouped_pool = ctx.enter_context(tc.tile_pool(name="grouped_pool", bufs=4))
-        packed_pool = ctx.enter_context(tc.tile_pool(name="packed_pool", bufs=4))
+        grouped_pool = ctx.enter_context(tc.tile_pool(name="grouped_pool", bufs=6))
+        packed_pool = ctx.enter_context(tc.tile_pool(name="packed_pool", bufs=8))
         sample_pool = ctx.enter_context(tc.tile_pool(name="sample_pool", bufs=2))
-        xt_pool = ctx.enter_context(tc.psum_pool(name="xt_pool", bufs=4))
-        acc_pool = ctx.enter_context(tc.psum_pool(name="acc_pool", bufs=2))
+        xt_pool = ctx.enter_context(tc.psum_pool(name="xt_pool", bufs=3))
+        out_pool = ctx.enter_context(tc.psum_pool(name="out_pool", bufs=N_HALVES))
+        mu_pool = ctx.enter_context(tc.psum_pool(name="mu_pool", bufs=1))
         ls_pool = ctx.enter_context(tc.psum_pool(name="ls_pool", bufs=1))
         eps_pool = ctx.enter_context(tc.psum_pool(name="eps_pool", bufs=1))
 
@@ -56,24 +59,42 @@ def tile_vae_pa_k_kernel(tc, h, W_mu_e, b_mu_e, W_ls_e, b_ls_e, eps_z, W_in_d, b
         eps_raw = keep.tile([P, LATENT], BF16)
         mu_rows = W_mu_e.rearrange("(c p e) k -> p c (e k)", p=P, e=2)
         ls_rows = W_ls_e.rearrange("(c p e) k -> p c (e k)", p=P, e=2)
+        d_rows = W_in_d.rearrange("(nb n) z -> n nb z", n=P)
         w_raw = {}
-        for g in range(Z_PASSES):
-            w_raw[g] = w_pool.tile([P, 2, 2, 2 * HIDDEN], BF16, name="w_raw")
-            nc.sync.dma_start(out=w_raw[g][:, 0, :, :], in_=mu_rows[:, 2 * g : 2 * g + 2, :])
-            nc.sync.dma_start(out=w_raw[g][:, 1, :, :], in_=ls_rows[:, 2 * g : 2 * g + 2, :])
-            if g == 0:
-                nc.sync.dma_start(out=bias_rows[0:32, :], in_=b_mu_e.rearrange("(c x) -> c x", x=2 * P))
-                nc.sync.dma_start(out=bias_rows[32:64, :], in_=b_ls_e.rearrange("(c x) -> c x", x=2 * P))
-                nc.sync.dma_start(out=b_in_row[0:1, :], in_=b_in_d.rearrange("(o n) -> o n", o=1))
+        d_raw = {}
+
+        def load_encoder(g):
+            w_raw[g] = w_pool.tile([P, 2, PACK, HIDDEN], BF16, name="w_raw")
+            for w, rows in enumerate((mu_rows, ls_rows)):
+                nc.sync.dma_start(
+                    out=w_raw[g][:, w, :, :].rearrange("p (c e) k -> p c (e k)", e=2),
+                    in_=rows[:, 2 * g : 2 * g + 2, :],
+                )
             if g % 4 == 0:
                 quarter = slice(g * K_PASS, (g + 4) * K_PASS)
                 nc.sync.dma_start(out=eps_raw[:, quarter], in_=eps_z[:, quarter])
-        d_raw = {}
-        for nb in range(N_BLOCKS):
-            d_raw[nb] = d_pool.tile([P, LATENT], BF16, name="d_raw")
-            for half in range(2):
-                cols = slice(half * LATENT // 2, (half + 1) * LATENT // 2)
-                nc.sync.dma_start(out=d_raw[nb][:, cols], in_=W_in_d[nb * P : (nb + 1) * P, cols])
+
+        def load_decoder(chunk):
+            quarter, n_half = divmod(chunk, N_HALVES)
+            d_raw[chunk] = d_pool.tile([P, PACK, CHUNK_PASSES * K_PASS], BF16, name="d_raw")
+            nc.sync.dma_start(
+                out=d_raw[chunk][:],
+                in_=d_rows[
+                    :,
+                    n_half * PACK : (n_half + 1) * PACK,
+                    quarter * CHUNK_PASSES * K_PASS : (quarter + 1) * CHUNK_PASSES * K_PASS,
+                ],
+            )
+
+        load_encoder(0)
+        nc.sync.dma_start(out=bias_rows[0:32, :], in_=b_mu_e.rearrange("(c x) -> c x", x=2 * P))
+        nc.sync.dma_start(out=bias_rows[32:64, :], in_=b_ls_e.rearrange("(c x) -> c x", x=2 * P))
+        nc.sync.dma_start(out=b_in_row[0:1, :], in_=b_in_d.rearrange("(o n) -> o n", o=1))
+        for i in range(ROUNDS):
+            if i + 1 < Z_PASSES:
+                load_encoder(i + 1)
+            if 0 <= i - LEAD < Z_PASSES and (i - LEAD) % 2 == 0:
+                load_decoder((i - LEAD) // 2)
 
         def transpose_unit(words, last_copy_on_vector):
             grouped = grouped_pool.tile([P, PACK * K_PASS], BF16, align_bytes=64)
@@ -82,8 +103,9 @@ def tile_vae_pa_k_kernel(tc, h, W_mu_e, b_mu_e, W_ls_e, b_ls_e, eps_z, W_in_d, b
                 xt = xt_pool.tile([P, 2, 2, P], F32)
                 for j in range(2):
                     for half in range(2):
-                        first = ((2 * bank + j) * 2 + half) * P
-                        nc.tensor.transpose(xt[:, j, half, :], words[:, first : first + P], ident[:])
+                        nc.tensor.transpose(
+                            xt[:, j, half, :], words[:, 2 * bank + j, half * P : (half + 1) * P], ident[:]
+                        )
                 copy_out = nc.vector.tensor_copy if (last_copy_on_vector and bank == 1) else nc.scalar.copy
                 copy_out(
                     out=grouped_words[:, 2 * bank : 2 * bank + 2, :, :],
@@ -97,22 +119,25 @@ def tile_vae_pa_k_kernel(tc, h, W_mu_e, b_mu_e, W_ls_e, b_ls_e, eps_z, W_in_d, b
             nc.vector.quantize_mx(out=codes[:].bitcast(FP8X4), scales=scales[:], in_=grouped[:])
             return codes, scales
 
-        def step_units(step):
-            if step < Z_PASSES:
-                return [w_raw[step][:, w, :, :].rearrange("p c x -> p (c x)").bitcast(F32) for w in range(2)]
-            nb, half = divmod(step - Z_PASSES, 2)
-            d_words = d_raw[nb][:].bitcast(F32)
-            return [d_words[:, (2 * half + r) * UNIT_WORDS : (2 * half + r + 1) * UNIT_WORDS] for r in range(2)]
+        def decoder_units(r):
+            chunk, second = divmod(r, 2)
+            quarter, n_half = divmod(chunk, N_HALVES)
+            return [(n_half, quarter * CHUNK_PASSES + 2 * second + m) for m in range(2)]
 
-        grouped_of = {}
-        packed_of = {}
+        w_grouped = {}
+        w_packed = {}
+        d_grouped = {}
+        d_packed = {}
 
-        def transposes(step):
-            units = step_units(step)
-            grouped_of[step] = [
-                transpose_unit(units[0], False),
-                transpose_unit(units[1], step >= Z_PASSES),
-            ]
+        def transpose_encoder(g):
+            w_grouped[g] = [transpose_unit(w_raw[g][:, w, :, :].bitcast(F32), False) for w in range(2)]
+
+        def transpose_decoder(r):
+            d_words = d_raw[r // 2][:].bitcast(F32)
+            d_grouped[r] = []
+            for m, (n_half, g) in enumerate(decoder_units(r)):
+                first = (g % CHUNK_PASSES) * 2 * P
+                d_grouped[r].append(transpose_unit(d_words[:, :, first : first + 2 * P], m == 1))
 
         h_words = h_raw[:].bitcast(F32)
         h_xt = xt_pool.tile([P, 2, 2, P], F32, tag="xt")
@@ -123,7 +148,7 @@ def tile_vae_pa_k_kernel(tc, h, W_mu_e, b_mu_e, W_ls_e, b_ls_e, eps_z, W_in_d, b
             out=h_grouped[:].bitcast(F32).rearrange("q (c half) -> q c half", half=2),
             in_=h_xt[:, 0, :, :].rearrange("q half c -> q c half"),
         )
-        transposes(0)
+        transpose_encoder(0)
         h_codes = keep.tile([P, P], U32, align_bytes=64)
         h_scales = keep.tile([P, P], U8, align_bytes=64)
         nc.vector.quantize_mx(out=h_codes[:].bitcast(FP8X4), scales=h_scales[:], in_=h_grouped[:])
@@ -146,7 +171,7 @@ def tile_vae_pa_k_kernel(tc, h, W_mu_e, b_mu_e, W_ls_e, b_ls_e, eps_z, W_in_d, b
             nc.tensor.matmul(out=b_in_flat, lhsT=ones[:], rhs=b_in_row[:, cols], start=True, stop=True)
             nc.vector.tensor_copy(out=b_in_all[:, cols], in_=b_in_flat)
 
-        packed_of[0] = [quantise_unit(grouped_of[0][0]), quantise_unit(grouped_of[0][1])]
+        w_packed[0] = [quantise_unit(w_grouped[0][0]), quantise_unit(w_grouped[0][1])]
 
         eps_words = eps_raw[:].bitcast(F32)
         z_codes = keep.tile([P, Z_PASSES, P], U32, align_bytes=64)
@@ -167,9 +192,9 @@ def tile_vae_pa_k_kernel(tc, h, W_mu_e, b_mu_e, W_ls_e, b_ls_e, eps_z, W_in_d, b
             for half in range(2):
                 first = (2 * g + half) * P
                 nc.tensor.transpose(eps_of[g][:, half, :], eps_words[:, first : first + P], ident[:])
-            mu_of[g] = acc_pool.tile([P, PACK, P], F32, name="mu_ps", tag="acc")
+            mu_of[g] = mu_pool.tile([P, PACK, P], F32, name="mu_ps")
             ls_of[g] = ls_pool.tile([P, PACK, P], F32, name="ls_ps")
-            for (codes, scales), ps in zip(packed_of[g], (mu_of[g], ls_of[g])):
+            for (codes, scales), ps in zip(w_packed[g], (mu_of[g], ls_of[g])):
                 for t in range(PACK):
                     cols = slice(t * P, (t + 1) * P)
                     nc.tensor.matmul_mx(
@@ -225,56 +250,53 @@ def tile_vae_pa_k_kernel(tc, h, W_mu_e, b_mu_e, W_ls_e, b_ls_e, eps_z, W_in_d, b
                 in_=z_grouped_of[g][:].rearrange("p b t -> p (b t)"),
             )
 
-        def decode(nb, half):
-            if nb not in out_ps:
-                if nb < 2:
-                    out_ps[nb] = acc_pool.tile([P, N_BLOCKS // 2, P], F32, name="out_ps", tag="acc")
-                else:
-                    out_ps[nb] = out_ps[nb - 2]
-            for r in range(2):
-                codes, scales = packed_of[Z_PASSES + 2 * nb + half][r]
-                for j in range(PACK):
-                    g = (2 * half + r) * PACK + j
-                    cols = slice(j * P, (j + 1) * P)
-                    nc.tensor.matmul_mx(
-                        out=out_ps[nb][:, nb // 2, :],
-                        lhsT=z_codes[:, g, :].bitcast(FP8X4),
-                        lhsT_scale=z_scales[:, g, :],
-                        rhs=codes[:, cols].bitcast(FP8X4),
-                        rhs_scale=scales[:, cols],
-                        start=(g == 0),
-                        stop=(g == Z_PASSES - 1),
-                    )
+        def decode(r):
+            for (codes, scales), (n_half, g) in zip(d_packed[r], decoder_units(r)):
+                if g == 0:
+                    out_ps[n_half] = out_pool.tile([P, N_TILE], F32, name="out_ps")
+                nc.tensor.matmul_mx(
+                    out=out_ps[n_half][:],
+                    lhsT=z_codes[:, g, :].bitcast(FP8X4),
+                    lhsT_scale=z_scales[:, g, :],
+                    rhs=codes[:].bitcast(FP8X4),
+                    rhs_scale=scales[:],
+                    start=(g == 0),
+                    stop=(g == Z_PASSES - 1),
+                )
+                if g == Z_PASSES - 1:
+                    finish(n_half)
 
-        def finish(nb):
-            cols = slice(nb * P, (nb + 1) * P)
-            nc.vector.tensor_tensor(
-                out=pre_tanh[:, cols], in0=out_ps[nb][:, nb // 2, :], in1=b_in_all[:, cols], op=ALU.add
-            )
+        def finish(n_half):
+            cols = slice(n_half * N_TILE, (n_half + 1) * N_TILE)
+            nc.vector.tensor_tensor(out=pre_tanh[:, cols], in0=out_ps[n_half][:], in1=b_in_all[:, cols], op=ALU.add)
             nc.scalar.activation(out=result[:, cols], in_=pre_tanh[:, cols], func=ACT.Tanh)
             nc.sync.dma_start(out=out[:, cols], in_=result[:, cols])
 
-        for i in range(STEPS):
-            sampling = 1 <= i <= Z_PASSES
-            if i + 1 < STEPS:
-                transposes(i + 1)
-            if sampling:
+        def is_pass(g):
+            return 0 <= g < Z_PASSES
+
+        for i in range(ROUNDS):
+            if is_pass(i + 1):
+                transpose_encoder(i + 1)
+            if is_pass(i - 1):
                 scale_noise(i - 1)
-            if 2 <= i <= Z_PASSES + 1:
+            if is_pass(i - 2):
                 quantise_z(i - 2)
-            if i < Z_PASSES:
-                encode(i)
-            else:
-                decode((i - Z_PASSES) // 2, (i - Z_PASSES) % 2)
-            if sampling:
+            if is_pass(i - 1):
                 add_mean(i - 1)
-            if i + 1 < STEPS:
-                first_unit = quantise_unit(grouped_of[i + 1][0])
-            if sampling:
+            if is_pass(i + 1):
+                first_unit = quantise_unit(w_grouped[i + 1][0])
+            if is_pass(i - 1):
                 regroup_z(i - 1)
-            if i + 1 < STEPS:
-                packed_of[i + 1] = [first_unit, quantise_unit(grouped_of[i + 1][1])]
-            if i < Z_PASSES:
+            if is_pass(i + 1):
+                w_packed[i + 1] = [first_unit, quantise_unit(w_grouped[i + 1][1])]
+            if is_pass(i - LEAD):
+                transpose_decoder(i - LEAD)
+            if is_pass(i):
+                encode(i)
+            if is_pass(i - LEAD - 1):
+                decode(i - LEAD - 1)
+            if is_pass(i - LEAD):
+                d_packed[i - LEAD] = [quantise_unit(grouped) for grouped in d_grouped[i - LEAD]]
+            if is_pass(i):
                 std_dev(i)
-            elif (i - Z_PASSES) % 2 == 1:
-                finish((i - Z_PASSES) // 2)

@@ -25,6 +25,7 @@ LEAD = 3
 ROUNDS = Z_PASSES + LEAD + 1
 W_BUFS = 6
 D_BUFS = 4
+CLOCK_COLS = 64
 
 FLOPS = 2 * P * (2 * HIDDEN * LATENT + LATENT * OUT)
 
@@ -39,11 +40,10 @@ def tile_vae_pa_k_kernel(tc, h, W_mu_e, b_mu_e, W_ls_e, b_ls_e, eps_z, W_in_d, b
         grouped_pool = ctx.enter_context(tc.tile_pool(name="grouped_pool", bufs=6))
         packed_pool = ctx.enter_context(tc.tile_pool(name="packed_pool", bufs=8))
         sample_pool = ctx.enter_context(tc.tile_pool(name="sample_pool", bufs=2))
-        xt_pool = ctx.enter_context(tc.psum_pool(name="xt_pool", bufs=3))
+        xt_pool = ctx.enter_context(tc.psum_pool(name="xt_pool", bufs=4))
         out_pool = ctx.enter_context(tc.psum_pool(name="out_pool", bufs=N_HALVES))
         mu_pool = ctx.enter_context(tc.psum_pool(name="mu_pool", bufs=1))
         ls_pool = ctx.enter_context(tc.psum_pool(name="ls_pool", bufs=1))
-        eps_pool = ctx.enter_context(tc.psum_pool(name="eps_pool", bufs=1))
 
         ident = keep.tile([P, P], F32)
         make_identity(nc, ident[:])
@@ -96,11 +96,15 @@ def tile_vae_pa_k_kernel(tc, h, W_mu_e, b_mu_e, W_ls_e, b_ls_e, eps_z, W_in_d, b
             if 0 <= i - LEAD < Z_PASSES and (i - LEAD) % 2 == 0:
                 load_decoder((i - LEAD) // 2)
 
-        def transpose_unit(words, last_copy_on_vector):
+        def transpose_unit(words, last_copy_on_vector, hold_clock):
             grouped = grouped_pool.tile([P, PACK * K_PASS], BF16, align_bytes=64)
             grouped_words = grouped[:].bitcast(F32).rearrange("q (j c half) -> q j c half", j=4, half=2)
             for bank in range(2):
                 xt = xt_pool.tile([P, 2, 2, P], F32)
+                if hold_clock:
+                    nc.tensor.matmul(
+                        out=xt[:, 0, 0, 0:CLOCK_COLS], lhsT=ident[:], rhs=ident[:, 0:CLOCK_COLS], start=True, stop=True
+                    )
                 for j in range(2):
                     for half in range(2):
                         nc.tensor.transpose(
@@ -130,14 +134,14 @@ def tile_vae_pa_k_kernel(tc, h, W_mu_e, b_mu_e, W_ls_e, b_ls_e, eps_z, W_in_d, b
         d_packed = {}
 
         def transpose_encoder(g):
-            w_grouped[g] = [transpose_unit(w_raw[g][:, w, :, :].bitcast(F32), False) for w in range(2)]
+            w_grouped[g] = [transpose_unit(w_raw[g][:, w, :, :].bitcast(F32), False, True) for w in range(2)]
 
-        def transpose_decoder(r):
+        def transpose_decoder(r, hold_clock):
             d_words = d_raw[r // 2][:].bitcast(F32)
             d_grouped[r] = []
             for m, (n_half, g) in enumerate(decoder_units(r)):
                 first = (g % CHUNK_PASSES) * 2 * P
-                d_grouped[r].append(transpose_unit(d_words[:, :, first : first + 2 * P], m == 1))
+                d_grouped[r].append(transpose_unit(d_words[:, :, first : first + 2 * P], m == 1, hold_clock))
 
         h_words = h_raw[:].bitcast(F32)
         h_xt = xt_pool.tile([P, 2, 2, P], F32, tag="xt")
@@ -188,10 +192,6 @@ def tile_vae_pa_k_kernel(tc, h, W_mu_e, b_mu_e, W_ls_e, b_ls_e, eps_z, W_in_d, b
         out_ps = {}
 
         def encode(g):
-            eps_of[g] = eps_pool.tile([P, 2, P], F32, name="eps_ps")
-            for half in range(2):
-                first = (2 * g + half) * P
-                nc.tensor.transpose(eps_of[g][:, half, :], eps_words[:, first : first + P], ident[:])
             mu_of[g] = mu_pool.tile([P, PACK, P], F32, name="mu_ps")
             ls_of[g] = ls_pool.tile([P, PACK, P], F32, name="ls_ps")
             for (codes, scales), ps in zip(w_packed[g], (mu_of[g], ls_of[g])):
@@ -206,6 +206,12 @@ def tile_vae_pa_k_kernel(tc, h, W_mu_e, b_mu_e, W_ls_e, b_ls_e, eps_z, W_in_d, b
                         start=True,
                         stop=True,
                     )
+
+        def transpose_noise(g):
+            eps_of[g] = xt_pool.tile([P, 2, 2, P], F32, name="eps_ps", tag="xt")
+            for half in range(2):
+                first = (2 * g + half) * P
+                nc.tensor.transpose(eps_of[g][:, 0, half, :], eps_words[:, first : first + P], ident[:])
 
         def std_dev(g):
             std_of[g] = sample_pool.tile([P, PACK, P], F32, name="std")
@@ -223,7 +229,7 @@ def tile_vae_pa_k_kernel(tc, h, W_mu_e, b_mu_e, W_ls_e, b_ls_e, eps_z, W_in_d, b
             nc.vector.tensor_tensor(
                 out=noise_of[g][:].rearrange("p (half e) b -> p half e b", e=2),
                 in0=std_of[g][:].rearrange("p (half e) b -> p half e b", e=2),
-                in1=eps_of[g][:].bitcast(BF16).rearrange("p half (b e) -> p half e b", e=2),
+                in1=eps_of[g][:, 0, :, :].bitcast(BF16).rearrange("p half (b e) -> p half e b", e=2),
                 op=ALU.mult,
             )
 
@@ -291,11 +297,13 @@ def tile_vae_pa_k_kernel(tc, h, W_mu_e, b_mu_e, W_ls_e, b_ls_e, eps_z, W_in_d, b
             if is_pass(i + 1):
                 w_packed[i + 1] = [first_unit, quantise_unit(w_grouped[i + 1][1])]
             if is_pass(i - LEAD):
-                transpose_decoder(i - LEAD)
+                transpose_decoder(i - LEAD, is_pass(i))
             if is_pass(i):
                 encode(i)
             if is_pass(i - LEAD - 1):
                 decode(i - LEAD - 1)
+            if is_pass(i):
+                transpose_noise(i)
             if is_pass(i - LEAD):
                 d_packed[i - LEAD] = [quantise_unit(grouped) for grouped in d_grouped[i - LEAD]]
             if is_pass(i):

from contextlib import ExitStack

import concourse.mybir as mybir
from concourse.masks import make_identity

F32 = mybir.dt.float32
BF16 = mybir.dt.bfloat16
U32 = mybir.dt.uint32
U8 = mybir.dt.uint8
FP8X4 = mybir.dt.float8_e4m3fn_x4
ACT = mybir.ActivationFunctionType
ALU = mybir.AluOpType

P = 128
PACK = 4
K_PASS = P * PACK
HIDDEN = 512
LATENT = 8192
OUT = 1024
Z_PASSES = LATENT // K_PASS
N_TILE = 512
N_HALVES = OUT // N_TILE
CHUNK_PASSES = 4
LEAD = 3
ROUNDS = Z_PASSES + LEAD + 1
W_BUFS = 6
D_BUFS = 4
CLOCK_COLS = 64

FLOPS = 2 * P * (2 * HIDDEN * LATENT + LATENT * OUT)


def tile_vae_pa_k_kernel(tc, h, W_mu_e, b_mu_e, W_ls_e, b_ls_e, eps_z, W_in_d, b_in_d, out):
    nc = tc.nc
    with ExitStack() as ctx:
        ctx.enter_context(tc.manual_schedule())
        keep = ctx.enter_context(tc.tile_pool(name="keep", bufs=1))
        w_pool = ctx.enter_context(tc.tile_pool(name="w_pool", bufs=W_BUFS))
        d_pool = ctx.enter_context(tc.tile_pool(name="d_pool", bufs=D_BUFS))
        grouped_pool = ctx.enter_context(tc.tile_pool(name="grouped_pool", bufs=6))
        packed_pool = ctx.enter_context(tc.tile_pool(name="packed_pool", bufs=8))
        sample_pool = ctx.enter_context(tc.tile_pool(name="sample_pool", bufs=2))
        xt_pool = ctx.enter_context(tc.psum_pool(name="xt_pool", bufs=4))
        out_pool = ctx.enter_context(tc.psum_pool(name="out_pool", bufs=N_HALVES))
        mu_pool = ctx.enter_context(tc.psum_pool(name="mu_pool", bufs=1))
        ls_pool = ctx.enter_context(tc.psum_pool(name="ls_pool", bufs=1))

        ident = keep.tile([P, P], F32)
        make_identity(nc, ident[:])
        ones = keep.tile([P, P], BF16)
        nc.vector.memset(ones[:], 1.0)
        bias_rows = keep.tile([P, 2 * P], BF16)
        nc.vector.memset(bias_rows[:], 0.0)
        b_in_row = keep.tile([P, OUT], BF16)
        nc.vector.memset(b_in_row[:], 0.0)

        h_raw = keep.tile([P, HIDDEN], BF16)
        nc.sync.dma_start(out=h_raw[:], in_=h[:, :])
        eps_raw = keep.tile([P, LATENT], BF16)
        mu_rows = W_mu_e.rearrange("(c p e) k -> p c (e k)", p=P, e=2)
        ls_rows = W_ls_e.rearrange("(c p e) k -> p c (e k)", p=P, e=2)
        d_rows = W_in_d.rearrange("(nb n) z -> n nb z", n=P)
        w_raw = {}
        d_raw = {}

        def load_encoder(g):
            w_raw[g] = w_pool.tile([P, 2, PACK, HIDDEN], BF16, name="w_raw")
            for w, rows in enumerate((mu_rows, ls_rows)):
                nc.sync.dma_start(
                    out=w_raw[g][:, w, :, :].rearrange("p (c e) k -> p c (e k)", e=2),
                    in_=rows[:, 2 * g : 2 * g + 2, :],
                )
            if g % 4 == 0:
                quarter = slice(g * K_PASS, (g + 4) * K_PASS)
                nc.sync.dma_start(out=eps_raw[:, quarter], in_=eps_z[:, quarter])

        def load_decoder(chunk):
            quarter, n_half = divmod(chunk, N_HALVES)
            d_raw[chunk] = d_pool.tile([P, PACK, CHUNK_PASSES * K_PASS], BF16, name="d_raw")
            nc.sync.dma_start(
                out=d_raw[chunk][:],
                in_=d_rows[
                    :,
                    n_half * PACK : (n_half + 1) * PACK,
                    quarter * CHUNK_PASSES * K_PASS : (quarter + 1) * CHUNK_PASSES * K_PASS,
                ],
            )

        load_encoder(0)
        nc.sync.dma_start(out=bias_rows[0:32, :], in_=b_mu_e.rearrange("(c x) -> c x", x=2 * P))
        nc.sync.dma_start(out=bias_rows[32:64, :], in_=b_ls_e.rearrange("(c x) -> c x", x=2 * P))
        nc.sync.dma_start(out=b_in_row[0:1, :], in_=b_in_d.rearrange("(o n) -> o n", o=1))
        for i in range(ROUNDS):
            if i + 1 < Z_PASSES:
                load_encoder(i + 1)
            if 0 <= i - LEAD < Z_PASSES and (i - LEAD) % 2 == 0:
                load_decoder((i - LEAD) // 2)

        def transpose_unit(words, last_copy_on_vector, hold_clock):
            grouped = grouped_pool.tile([P, PACK * K_PASS], BF16, align_bytes=64)
            grouped_words = grouped[:].bitcast(F32).rearrange("q (j c half) -> q j c half", j=4, half=2)
            for bank in range(2):
                xt = xt_pool.tile([P, 2, 2, P], F32)
                if hold_clock:
                    nc.tensor.matmul(
                        out=xt[:, 0, 0, 0:CLOCK_COLS], lhsT=ident[:], rhs=ident[:, 0:CLOCK_COLS], start=True, stop=True
                    )
                for j in range(2):
                    for half in range(2):
                        nc.tensor.transpose(
                            xt[:, j, half, :], words[:, 2 * bank + j, half * P : (half + 1) * P], ident[:]
                        )
                copy_out = nc.vector.tensor_copy if (last_copy_on_vector and bank == 1) else nc.scalar.copy
                copy_out(
                    out=grouped_words[:, 2 * bank : 2 * bank + 2, :, :],
                    in_=xt[:].rearrange("q j half c -> q j c half"),
                )
            return grouped

        def quantise_unit(grouped):
            codes = packed_pool.tile([P, K_PASS], U32, align_bytes=64)
            scales = packed_pool.tile([P, K_PASS], U8, align_bytes=64)
            nc.vector.quantize_mx(out=codes[:].bitcast(FP8X4), scales=scales[:], in_=grouped[:])
            return codes, scales

        def decoder_units(r):
            chunk, second = divmod(r, 2)
            quarter, n_half = divmod(chunk, N_HALVES)
            return [(n_half, quarter * CHUNK_PASSES + 2 * second + m) for m in range(2)]

        w_grouped = {}
        w_packed = {}
        d_grouped = {}
        d_packed = {}

        def transpose_encoder(g):
            w_grouped[g] = [transpose_unit(w_raw[g][:, w, :, :].bitcast(F32), False, True) for w in range(2)]

        def transpose_decoder(r, hold_clock):
            d_words = d_raw[r // 2][:].bitcast(F32)
            d_grouped[r] = []
            for m, (n_half, g) in enumerate(decoder_units(r)):
                first = (g % CHUNK_PASSES) * 2 * P
                d_grouped[r].append(transpose_unit(d_words[:, :, first : first + 2 * P], m == 1, hold_clock))

        h_words = h_raw[:].bitcast(F32)
        h_xt = xt_pool.tile([P, 2, 2, P], F32, tag="xt")
        for half in range(2):
            nc.tensor.transpose(h_xt[:, 0, half, :], h_words[:, half * P : (half + 1) * P], ident[:])
        h_grouped = keep.tile([P, K_PASS], BF16, align_bytes=64)
        nc.vector.tensor_copy(
            out=h_grouped[:].bitcast(F32).rearrange("q (c half) -> q c half", half=2),
            in_=h_xt[:, 0, :, :].rearrange("q half c -> q c half"),
        )
        transpose_encoder(0)
        h_codes = keep.tile([P, P], U32, align_bytes=64)
        h_scales = keep.tile([P, P], U8, align_bytes=64)
        nc.vector.quantize_mx(out=h_codes[:].bitcast(FP8X4), scales=h_scales[:], in_=h_grouped[:])

        bias_xt = xt_pool.tile([P, 2, 2, P], F32, tag="xt")
        nc.tensor.transpose(bias_xt[:, 0, 0, :], bias_rows[:].bitcast(F32), ident[:])
        bias_pairs = bias_xt[:, 0, 0, :].bitcast(BF16)
        b_mu_cols = keep.tile([P, PACK * Z_PASSES], F32)
        nc.vector.tensor_copy(out=b_mu_cols[:], in_=bias_pairs[:, 0 : PACK * Z_PASSES])
        half_b_ls_cols = keep.tile([P, PACK * Z_PASSES], F32)
        nc.vector.tensor_scalar_mul(
            out=half_b_ls_cols[:], in0=bias_pairs[:, PACK * Z_PASSES : 2 * PACK * Z_PASSES], scalar1=0.5
        )

        b_in_all = keep.tile([P, OUT], F32)
        for half in range(2):
            cols = slice(half * K_PASS, (half + 1) * K_PASS)
            b_in_ps = xt_pool.tile([P, 2, 2, P], F32, tag="xt")
            b_in_flat = b_in_ps[:].rearrange("q j half c -> q (j half c)")
            nc.tensor.matmul(out=b_in_flat, lhsT=ones[:], rhs=b_in_row[:, cols], start=True, stop=True)
            nc.vector.tensor_copy(out=b_in_all[:, cols], in_=b_in_flat)

        w_packed[0] = [quantise_unit(w_grouped[0][0]), quantise_unit(w_grouped[0][1])]

        eps_words = eps_raw[:].bitcast(F32)
        z_codes = keep.tile([P, Z_PASSES, P], U32, align_bytes=64)
        z_scales = keep.tile([P, Z_PASSES, P], U8, align_bytes=64)
        pre_tanh = keep.tile([P, OUT], F32)
        result = keep.tile([P, OUT], F32)
        mu_of = {}
        ls_of = {}
        eps_of = {}
        std_of = {}
        noise_of = {}
        planes_of = {}
        z_grouped_of = {}
        out_ps = {}

        def encode(g):
            mu_of[g] = mu_pool.tile([P, PACK, P], F32, name="mu_ps")
            ls_of[g] = ls_pool.tile([P, PACK, P], F32, name="ls_ps")
            for (codes, scales), ps in zip(w_packed[g], (mu_of[g], ls_of[g])):
                for t in range(PACK):
                    cols = slice(t * P, (t + 1) * P)
                    nc.tensor.matmul_mx(
                        out=ps[:, t, :],
                        lhsT=codes[:, cols].bitcast(FP8X4),
                        lhsT_scale=scales[:, cols],
                        rhs=h_codes[:].bitcast(FP8X4),
                        rhs_scale=h_scales[:],
                        start=True,
                        stop=True,
                    )

        def transpose_noise(g):
            eps_of[g] = xt_pool.tile([P, 2, 2, P], F32, name="eps_ps", tag="xt")
            for half in range(2):
                first = (2 * g + half) * P
                nc.tensor.transpose(eps_of[g][:, 0, half, :], eps_words[:, first : first + P], ident[:])

        def std_dev(g):
            std_of[g] = sample_pool.tile([P, PACK, P], F32, name="std")
            for t in range(PACK):
                nc.scalar.activation(
                    out=std_of[g][:, t, :],
                    in_=ls_of[g][:, t, :],
                    func=ACT.Exp,
                    bias=half_b_ls_cols[:, PACK * g + t : PACK * g + t + 1],
                    scale=0.5,
                )

        def scale_noise(g):
            noise_of[g] = sample_pool.tile([P, PACK, P], F32, name="noise")
            nc.vector.tensor_tensor(
                out=noise_of[g][:].rearrange("p (half e) b -> p half e b", e=2),
                in0=std_of[g][:].rearrange("p (half e) b -> p half e b", e=2),
                in1=eps_of[g][:, 0, :, :].bitcast(BF16).rearrange("p half (b e) -> p half e b", e=2),
                op=ALU.mult,
            )

        def add_mean(g):
            planes_of[g] = sample_pool.tile([P, PACK, P], BF16, name="z_planes")
            for t in range(PACK):
                nc.vector.scalar_tensor_tensor(
                    out=planes_of[g][:, t, :],
                    in0=mu_of[g][:, t, :],
                    scalar=b_mu_cols[:, PACK * g + t : PACK * g + t + 1],
                    in1=noise_of[g][:, t, :],
                    op0=ALU.add,
                    op1=ALU.add,
                )

        def regroup_z(g):
            z_grouped_of[g] = sample_pool.tile([P, P, PACK], BF16, name="z_grouped", align_bytes=64)
            nc.vector.tensor_copy(out=z_grouped_of[g][:], in_=planes_of[g][:].rearrange("p t b -> p b t"))

        def quantise_z(g):
            nc.vector.quantize_mx(
                out=z_codes[:, g, :].bitcast(FP8X4),
                scales=z_scales[:, g, :],
                in_=z_grouped_of[g][:].rearrange("p b t -> p (b t)"),
            )

        def decode(r):
            for (codes, scales), (n_half, g) in zip(d_packed[r], decoder_units(r)):
                if g == 0:
                    out_ps[n_half] = out_pool.tile([P, N_TILE], F32, name="out_ps")
                nc.tensor.matmul_mx(
                    out=out_ps[n_half][:],
                    lhsT=z_codes[:, g, :].bitcast(FP8X4),
                    lhsT_scale=z_scales[:, g, :],
                    rhs=codes[:].bitcast(FP8X4),
                    rhs_scale=scales[:],
                    start=(g == 0),
                    stop=(g == Z_PASSES - 1),
                )
                if g == Z_PASSES - 1:
                    finish(n_half)

        def finish(n_half):
            cols = slice(n_half * N_TILE, (n_half + 1) * N_TILE)
            nc.vector.tensor_tensor(out=pre_tanh[:, cols], in0=out_ps[n_half][:], in1=b_in_all[:, cols], op=ALU.add)
            nc.scalar.activation(out=result[:, cols], in_=pre_tanh[:, cols], func=ACT.Tanh)
            nc.sync.dma_start(out=out[:, cols], in_=result[:, cols])

        def is_pass(g):
            return 0 <= g < Z_PASSES

        for i in range(ROUNDS):
            if is_pass(i + 1):
                transpose_encoder(i + 1)
            if is_pass(i - 1):
                scale_noise(i - 1)
            if is_pass(i - 2):
                quantise_z(i - 2)
            if is_pass(i - 1):
                add_mean(i - 1)
            if is_pass(i + 1):
                first_unit = quantise_unit(w_grouped[i + 1][0])
            if is_pass(i - 1):
                regroup_z(i - 1)
            if is_pass(i + 1):
                w_packed[i + 1] = [first_unit, quantise_unit(w_grouped[i + 1][1])]
            if is_pass(i - LEAD):
                transpose_decoder(i - LEAD, is_pass(i))
            if is_pass(i):
                encode(i)
            if is_pass(i - LEAD - 1):
                decode(i - LEAD - 1)
            if is_pass(i):
                transpose_noise(i)
            if is_pass(i - LEAD):
                d_packed[i - LEAD] = [quantise_unit(grouped) for grouped in d_grouped[i - LEAD]]
            if is_pass(i):
                std_dev(i)
